import numpy as np
import ml_dtypes

BF16 = ml_dtypes.bfloat16


def bf(x):
    return np.asarray(x, np.float32).astype(BF16)


def f32(x):
    return np.asarray(x, np.float32)


def f64(x):
    return np.asarray(x).astype(np.float64)


def striped(idx):
    return np.tile(idx.reshape(-1, 16).T, (8, 1))


C, S, P, L, M, N = 768, 1024, 512, 4, 256, 2048
SLOPE = 0.01


def leaky(v):
    return np.maximum(v, SLOPE * v)


def setup_inputs():
    return {
        "x": f32(np.random.standard_normal((C, S))),
        "w_pool": bf(0.5 * np.random.standard_normal((C, C)) / np.sqrt(C)),
        "b_pool": f32(0.3 * np.random.standard_normal((C, 1))),
        "w_cls": bf(np.random.standard_normal((C, M)) / np.sqrt(C)),
        "b_cls": f32(0.3 * np.random.standard_normal((M, 1))),
        "offs": striped(np.random.permutation(np.tile(np.arange(S), 2))[:N]),
    }


def reference(x, w_pool, b_pool, w_cls, b_cls, offs):
    idx = offs[:16].T.reshape(-1)
    pooled = f64(x)[:, idx].reshape(C, L, P).sum(axis=1)
    hid = leaky(f64(w_pool).T @ pooled + f64(b_pool))
    return leaky(f64(w_cls).T @ hid + f64(b_cls))

@@ -1,0 +1,86 @@
+import concourse.mybir as mybir
+
+C, S, P, L, M, N = 768, 1024, 512, 4, 256, 2048
+SLOPE = 0.01
+PARTS = 128
+C_BLOCKS = C // PARTS
+M_BLOCKS = M // PARTS
+PIECE = P // 16
+FLOPS = 2 * C * C * P + 2 * C * M * P
+
+F32 = mybir.dt.float32
+BF16 = mybir.dt.bfloat16
+U16 = mybir.dt.uint16
+ADD = mybir.AluOpType.add
+MULT = mybir.AluOpType.mult
+MAX = mybir.AluOpType.max
+IDENTITY = mybir.ActivationFunctionType.Identity
+
+
+def tile_myclassifier_kernel(tc, x, w_pool, b_pool, w_cls, b_cls, offs, out):
+    nc = tc.nc
+    with (
+        tc.tile_pool(name="held", bufs=1) as held,
+        tc.tile_pool(name="sums", bufs=4) as sums,
+        tc.tile_pool(name="work", bufs=2) as work,
+        tc.psum_pool(name="psum", bufs=1) as psum,
+    ):
+        offsets = held.tile([PARTS, N // 16], U16, name="offsets")
+        nc.sync.dma_start(offsets[:], offs)
+        tokens = []
+        for cb in range(C_BLOCKS):
+            block = held.tile([PARTS, S], F32, name=f"tokens{cb}")
+            nc.sync.dma_start(block[:], x[cb * PARTS : (cb + 1) * PARTS, :])
+            tokens.append(block)
+        w_pool_sb = held.tile([PARTS, C_BLOCKS, C], BF16, name="w_pool_sb")
+        nc.scalar.dma_start(w_pool_sb[:], w_pool.rearrange("(cb p) d -> p cb d", p=PARTS))
+        w_cls_sb = held.tile([PARTS, C_BLOCKS, M], BF16, name="w_cls_sb")
+        nc.scalar.dma_start(w_cls_sb[:], w_cls.rearrange("(db p) m -> p db m", p=PARTS))
+        b_pool_sb = held.tile([PARTS, C_BLOCKS], F32, name="b_pool_sb")
+        b_cls_sb = held.tile([PARTS, M_BLOCKS], F32, name="b_cls_sb")
+        with nc.allow_non_contiguous_dma(reason="a bias value for each partition"):
+            nc.scalar.dma_start(b_pool_sb[:], b_pool.rearrange("(db p) one -> p (db one)", p=PARTS))
+            nc.scalar.dma_start(b_cls_sb[:], b_cls.rearrange("(mb p) one -> p (mb one)", p=PARTS))
+
+        hid_ps = [psum.tile([PARTS, P], F32, name=f"hid_ps{db}") for db in range(C_BLOCKS)]
+        out_ps = [psum.tile([PARTS, P], F32, name=f"out_ps{mb}") for mb in range(M_BLOCKS)]
+
+        for cb in range(C_BLOCKS):
+            pooled = sums.tile([PARTS, P], F32, name="pooled")
+            nc.vector.tensor_copy(pooled[:], tokens[cb][:].indirect(offsets[:, 0:PIECE]))
+            for l in range(1, L):
+                shorter = pooled
+                pooled = sums.tile([PARTS, P], F32, name="pooled")
+                picked = tokens[cb][:].indirect(offsets[:, l * PIECE : (l + 1) * PIECE])
+                nc.vector.tensor_tensor(pooled[:], picked, shorter[:], ADD)
+            pooled_bf = work.tile([PARTS, P], BF16, name="pooled_bf")
+            nc.scalar.copy(pooled_bf[:], pooled[:])
+            for db in range(C_BLOCKS):
+                nc.tensor.matmul(
+                    hid_ps[db][:],
+                    w_pool_sb[:, cb, db * PARTS : (db + 1) * PARTS],
+                    pooled_bf[:],
+                    start=(cb == 0),
+                    stop=(cb == C_BLOCKS - 1),
+                )
+
+        for db in range(C_BLOCKS):
+            hid_pre = work.tile([PARTS, P], F32, name="hid_pre")
+            nc.scalar.activation(hid_pre[:], hid_ps[db][:], IDENTITY, bias=b_pool_sb[:, db : db + 1])
+            hid_bf = work.tile([PARTS, P], BF16, name="hid_bf")
+            nc.vector.scalar_tensor_tensor(hid_bf[:], hid_pre[:], SLOPE, hid_pre[:], MULT, MAX)
+            for mb in range(M_BLOCKS):
+                nc.tensor.matmul(
+                    out_ps[mb][:],
+                    w_cls_sb[:, db, mb * PARTS : (mb + 1) * PARTS],
+                    hid_bf[:],
+                    start=(db == 0),
+                    stop=(db == C_BLOCKS - 1),
+                )
+
+        for mb in range(M_BLOCKS):
+            out_pre = work.tile([PARTS, P], F32, name="out_pre")
+            nc.scalar.activation(out_pre[:], out_ps[mb][:], IDENTITY, bias=b_cls_sb[:, mb : mb + 1])
+            out_sb = work.tile([PARTS, P], F32, name="out_sb")
+            nc.vector.scalar_tensor_tensor(out_sb[:], out_pre[:], SLOPE, out_pre[:], MULT, MAX)
+            nc.sync.dma_start(out[mb * PARTS : (mb + 1) * PARTS, :], out_sb[:])

@@ -21,7 +21,7 @@ def tile_myclassifier_kernel(tc, x, w_pool, b_pool, w_cls, b_cls, offs, out):
     nc = tc.nc
     with (
         tc.tile_pool(name="held", bufs=1) as held,
-        tc.tile_pool(name="sums", bufs=4) as sums,
+        tc.tile_pool(name="sums", bufs=8) as sums,
         tc.tile_pool(name="work", bufs=2) as work,
         tc.psum_pool(name="psum", bufs=1) as psum,
     ):
@@ -45,24 +45,29 @@ def tile_myclassifier_kernel(tc, x, w_pool, b_pool, w_cls, b_cls, offs, out):
         hid_ps = [psum.tile([PARTS, P], F32, name=f"hid_ps{db}") for db in range(C_BLOCKS)]
         out_ps = [psum.tile([PARTS, P], F32, name=f"out_ps{mb}") for mb in range(M_BLOCKS)]
 
-        for cb in range(C_BLOCKS):
-            pooled = sums.tile([PARTS, P], F32, name="pooled")
-            nc.vector.tensor_copy(pooled[:], tokens[cb][:].indirect(offsets[:, 0:PIECE]))
+        for first in range(0, C_BLOCKS, 2):
+            pair = (first, first + 1)
+            pooled = {}
+            for cb in pair:
+                pooled[cb] = sums.tile([PARTS, P], F32, name="pooled")
+                nc.vector.tensor_copy(pooled[cb][:], tokens[cb][:].indirect(offsets[:, 0:PIECE]))
             for l in range(1, L):
-                shorter = pooled
-                pooled = sums.tile([PARTS, P], F32, name="pooled")
-                picked = tokens[cb][:].indirect(offsets[:, l * PIECE : (l + 1) * PIECE])
-                nc.vector.tensor_tensor(pooled[:], picked, shorter[:], ADD)
-            pooled_bf = work.tile([PARTS, P], BF16, name="pooled_bf")
-            nc.scalar.copy(pooled_bf[:], pooled[:])
-            for db in range(C_BLOCKS):
-                nc.tensor.matmul(
-                    hid_ps[db][:],
-                    w_pool_sb[:, cb, db * PARTS : (db + 1) * PARTS],
-                    pooled_bf[:],
-                    start=(cb == 0),
-                    stop=(cb == C_BLOCKS - 1),
-                )
+                for cb in pair:
+                    shorter = pooled[cb]
+                    pooled[cb] = sums.tile([PARTS, P], F32, name="pooled")
+                    picked = tokens[cb][:].indirect(offsets[:, l * PIECE : (l + 1) * PIECE])
+                    nc.vector.tensor_tensor(pooled[cb][:], picked, shorter[:], ADD)
+            for cb in pair:
+                pooled_bf = work.tile([PARTS, P], BF16, name="pooled_bf")
+                nc.scalar.copy(pooled_bf[:], pooled[cb][:])
+                for db in range(C_BLOCKS):
+                    nc.tensor.matmul(
+                        hid_ps[db][:],
+                        w_pool_sb[:, cb, db * PARTS : (db + 1) * PARTS],
+                        pooled_bf[:],
+                        start=(cb == 0),
+                        stop=(cb == C_BLOCKS - 1),
+                    )
 
         for db in range(C_BLOCKS):
             hid_pre = work.tile([PARTS, P], F32, name="hid_pre")

@@ -45,29 +45,31 @@ def tile_myclassifier_kernel(tc, x, w_pool, b_pool, w_cls, b_cls, offs, out):
         hid_ps = [psum.tile([PARTS, P], F32, name=f"hid_ps{db}") for db in range(C_BLOCKS)]
         out_ps = [psum.tile([PARTS, P], F32, name=f"out_ps{mb}") for mb in range(M_BLOCKS)]
 
-        for first in range(0, C_BLOCKS, 2):
-            pair = (first, first + 1)
-            pooled = {}
-            for cb in pair:
-                pooled[cb] = sums.tile([PARTS, P], F32, name="pooled")
-                nc.vector.tensor_copy(pooled[cb][:], tokens[cb][:].indirect(offsets[:, 0:PIECE]))
-            for l in range(1, L):
-                for cb in pair:
+        pooled = {}
+        for step in range(2 * C_BLOCKS + 2):
+            for cb in (step // 2 - 1, step // 2):
+                if cb < 0 or cb >= C_BLOCKS:
+                    continue
+                l = step - 2 * cb
+                picked = tokens[cb][:].indirect(offsets[:, l * PIECE : (l + 1) * PIECE])
+                if l == 0:
+                    pooled[cb] = sums.tile([PARTS, P], F32, name="pooled")
+                    nc.vector.tensor_copy(pooled[cb][:], picked)
+                else:
                     shorter = pooled[cb]
                     pooled[cb] = sums.tile([PARTS, P], F32, name="pooled")
-                    picked = tokens[cb][:].indirect(offsets[:, l * PIECE : (l + 1) * PIECE])
                     nc.vector.tensor_tensor(pooled[cb][:], picked, shorter[:], ADD)
-            for cb in pair:
-                pooled_bf = work.tile([PARTS, P], BF16, name="pooled_bf")
-                nc.scalar.copy(pooled_bf[:], pooled[cb][:])
-                for db in range(C_BLOCKS):
-                    nc.tensor.matmul(
-                        hid_ps[db][:],
-                        w_pool_sb[:, cb, db * PARTS : (db + 1) * PARTS],
-                        pooled_bf[:],
-                        start=(cb == 0),
-                        stop=(cb == C_BLOCKS - 1),
-                    )
+                if l == L - 1:
+                    pooled_bf = work.tile([PARTS, P], BF16, name="pooled_bf")
+                    nc.scalar.copy(pooled_bf[:], pooled[cb][:])
+                    for db in range(C_BLOCKS):
+                        nc.tensor.matmul(
+                            hid_ps[db][:],
+                            w_pool_sb[:, cb, db * PARTS : (db + 1) * PARTS],
+                            pooled_bf[:],
+                            start=(cb == 0),
+                            stop=(cb == C_BLOCKS - 1),
+                        )
 
         for db in range(C_BLOCKS):
             hid_pre = work.tile([PARTS, P], F32, name="hid_pre")

@@ -22,54 +22,51 @@ def tile_myclassifier_kernel(tc, x, w_pool, b_pool, w_cls, b_cls, offs, out):
     with (
         tc.tile_pool(name="held", bufs=1) as held,
         tc.tile_pool(name="sums", bufs=8) as sums,
-        tc.tile_pool(name="work", bufs=2) as work,
+        tc.tile_pool(name="work", bufs=6) as work,
         tc.psum_pool(name="psum", bufs=1) as psum,
     ):
         offsets = held.tile([PARTS, N // 16], U16, name="offsets")
         nc.sync.dma_start(offsets[:], offs)
-        tokens = []
-        for cb in range(C_BLOCKS):
-            block = held.tile([PARTS, S], F32, name=f"tokens{cb}")
-            nc.sync.dma_start(block[:], x[cb * PARTS : (cb + 1) * PARTS, :])
-            tokens.append(block)
+        tokens = [held.tile([PARTS, S], F32, name=f"tokens{cb}") for cb in range(C_BLOCKS)]
         w_pool_sb = held.tile([PARTS, C_BLOCKS, C], BF16, name="w_pool_sb")
-        nc.scalar.dma_start(w_pool_sb[:], w_pool.rearrange("(cb p) d -> p cb d", p=PARTS))
         w_cls_sb = held.tile([PARTS, C_BLOCKS, M], BF16, name="w_cls_sb")
-        nc.scalar.dma_start(w_cls_sb[:], w_cls.rearrange("(db p) m -> p db m", p=PARTS))
         b_pool_sb = held.tile([PARTS, C_BLOCKS], F32, name="b_pool_sb")
         b_cls_sb = held.tile([PARTS, M_BLOCKS], F32, name="b_cls_sb")
+        for cb in range(C_BLOCKS):
+            nc.sync.dma_start(tokens[cb][:], x[cb * PARTS : (cb + 1) * PARTS, :])
+            if cb == 1:
+                nc.sync.dma_start(w_pool_sb[:], w_pool.rearrange("(cb p) d -> p cb d", p=PARTS))
+        nc.sync.dma_start(w_cls_sb[:], w_cls.rearrange("(db p) m -> p db m", p=PARTS))
         with nc.allow_non_contiguous_dma(reason="a bias value for each partition"):
-            nc.scalar.dma_start(b_pool_sb[:], b_pool.rearrange("(db p) one -> p (db one)", p=PARTS))
-            nc.scalar.dma_start(b_cls_sb[:], b_cls.rearrange("(mb p) one -> p (mb one)", p=PARTS))
+            nc.sync.dma_start(b_pool_sb[:], b_pool.rearrange("(db p) one -> p (db one)", p=PARTS))
+            nc.sync.dma_start(b_cls_sb[:], b_cls.rearrange("(mb p) one -> p (mb one)", p=PARTS))
 
         hid_ps = [psum.tile([PARTS, P], F32, name=f"hid_ps{db}") for db in range(C_BLOCKS)]
         out_ps = [psum.tile([PARTS, P], F32, name=f"out_ps{mb}") for mb in range(M_BLOCKS)]
 
-        pooled = {}
-        for step in range(2 * C_BLOCKS + 2):
-            for cb in (step // 2 - 1, step // 2):
-                if cb < 0 or cb >= C_BLOCKS:
-                    continue
-                l = step - 2 * cb
-                picked = tokens[cb][:].indirect(offsets[:, l * PIECE : (l + 1) * PIECE])
-                if l == 0:
-                    pooled[cb] = sums.tile([PARTS, P], F32, name="pooled")
-                    nc.vector.tensor_copy(pooled[cb][:], picked)
-                else:
+        for first in range(0, C_BLOCKS, 2):
+            pair = (first, first + 1)
+            pooled = {}
+            for cb in pair:
+                pooled[cb] = sums.tile([PARTS, P], F32, name="pooled")
+                nc.vector.tensor_copy(pooled[cb][:], tokens[cb][:].indirect(offsets[:, 0:PIECE]))
+            for l in range(1, L):
+                for cb in pair:
                     shorter = pooled[cb]
                     pooled[cb] = sums.tile([PARTS, P], F32, name="pooled")
+                    picked = tokens[cb][:].indirect(offsets[:, l * PIECE : (l + 1) * PIECE])
                     nc.vector.tensor_tensor(pooled[cb][:], picked, shorter[:], ADD)
-                if l == L - 1:
-                    pooled_bf = work.tile([PARTS, P], BF16, name="pooled_bf")
-                    nc.scalar.copy(pooled_bf[:], pooled[cb][:])
-                    for db in range(C_BLOCKS):
-                        nc.tensor.matmul(
-                            hid_ps[db][:],
-                            w_pool_sb[:, cb, db * PARTS : (db + 1) * PARTS],
-                            pooled_bf[:],
-                            start=(cb == 0),
-                            stop=(cb == C_BLOCKS - 1),
-                        )
+            for cb in pair:
+                pooled_bf = work.tile([PARTS, P], BF16, name="pooled_bf")
+                nc.scalar.copy(pooled_bf[:], pooled[cb][:])
+                for db in range(C_BLOCKS):
+                    nc.tensor.matmul(
+                        hid_ps[db][:],
+                        w_pool_sb[:, cb, db * PARTS : (db + 1) * PARTS],
+                        pooled_bf[:],
+                        start=(cb == 0),
+                        stop=(cb == C_BLOCKS - 1),
+                    )
 
         for db in range(C_BLOCKS):
             hid_pre = work.tile([PARTS, P], F32, name="hid_pre")

@@ -56,14 +56,16 @@ def tile_myclassifier_kernel(tc, x, w_pool, b_pool, w_cls, b_cls, offs, out):
                     pooled[cb] = sums.tile([PARTS, P], F32, name="pooled")
                     picked = tokens[cb][:].indirect(offsets[:, l * PIECE : (l + 1) * PIECE])
                     nc.vector.tensor_tensor(pooled[cb][:], picked, shorter[:], ADD)
+            pooled_bf = {}
             for cb in pair:
-                pooled_bf = work.tile([PARTS, P], BF16, name="pooled_bf")
-                nc.scalar.copy(pooled_bf[:], pooled[cb][:])
-                for db in range(C_BLOCKS):
+                pooled_bf[cb] = work.tile([PARTS, P], BF16, name="pooled_bf")
+                nc.scalar.copy(pooled_bf[cb][:], pooled[cb][:])
+            for db in range(C_BLOCKS):
+                for cb in pair:
                     nc.tensor.matmul(
                         hid_ps[db][:],
                         w_pool_sb[:, cb, db * PARTS : (db + 1) * PARTS],
-                        pooled_bf[:],
+                        pooled_bf[cb][:],
                         start=(cb == 0),
                         stop=(cb == C_BLOCKS - 1),
                     )

@@ -16,6 +16,8 @@ MULT = mybir.AluOpType.mult
 MAX = mybir.AluOpType.max
 IDENTITY = mybir.ActivationFunctionType.Identity
 
+CHUNKS = ((0, 384), (384, 512))
+
 
 def tile_myclassifier_kernel(tc, x, w_pool, b_pool, w_cls, b_cls, offs, out):
     nc = tc.nc
@@ -41,52 +43,57 @@ def tile_myclassifier_kernel(tc, x, w_pool, b_pool, w_cls, b_cls, offs, out):
             nc.sync.dma_start(b_pool_sb[:], b_pool.rearrange("(db p) one -> p (db one)", p=PARTS))
             nc.sync.dma_start(b_cls_sb[:], b_cls.rearrange("(mb p) one -> p (mb one)", p=PARTS))
 
-        hid_ps = [psum.tile([PARTS, P], F32, name=f"hid_ps{db}") for db in range(C_BLOCKS)]
-        out_ps = [psum.tile([PARTS, P], F32, name=f"out_ps{mb}") for mb in range(M_BLOCKS)]
+        for lo, hi in CHUNKS:
+            width = hi - lo
+            hid_ps = [psum.tile([PARTS, width], F32, name=f"hid_ps{db}") for db in range(C_BLOCKS)]
+            out_ps = [psum.tile([PARTS, width], F32, name=f"out_ps{mb}") for mb in range(M_BLOCKS)]
 
-        for first in range(0, C_BLOCKS, 2):
-            pair = (first, first + 1)
-            pooled = {}
-            for cb in pair:
-                pooled[cb] = sums.tile([PARTS, P], F32, name="pooled")
-                nc.vector.tensor_copy(pooled[cb][:], tokens[cb][:].indirect(offsets[:, 0:PIECE]))
-            for l in range(1, L):
+            for first in range(0, C_BLOCKS, 2):
+                pair = (first, first + 1)
+                pooled = {}
                 for cb in pair:
-                    shorter = pooled[cb]
-                    pooled[cb] = sums.tile([PARTS, P], F32, name="pooled")
-                    picked = tokens[cb][:].indirect(offsets[:, l * PIECE : (l + 1) * PIECE])
-                    nc.vector.tensor_tensor(pooled[cb][:], picked, shorter[:], ADD)
-            pooled_bf = {}
-            for cb in pair:
-                pooled_bf[cb] = work.tile([PARTS, P], BF16, name="pooled_bf")
-                nc.scalar.copy(pooled_bf[cb][:], pooled[cb][:])
+                    pooled[cb] = sums.tile([PARTS, width], F32, name="pooled")
+                    picked = tokens[cb][:].indirect(offsets[:, lo // 16 : hi // 16])
+                    nc.vector.tensor_copy(pooled[cb][:], picked)
+                for l in range(1, L):
+                    for cb in pair:
+                        shorter = pooled[cb]
+                        pooled[cb] = sums.tile([PARTS, width], F32, name="pooled")
+                        picked = tokens[cb][:].indirect(
+                            offsets[:, l * PIECE + lo // 16 : l * PIECE + hi // 16]
+                        )
+                        nc.vector.tensor_tensor(pooled[cb][:], picked, shorter[:], ADD)
+                pooled_bf = {}
+                for cb in pair:
+                    pooled_bf[cb] = work.tile([PARTS, width], BF16, name="pooled_bf")
+                    nc.scalar.copy(pooled_bf[cb][:], pooled[cb][:])
+                for db in range(C_BLOCKS):
+                    for cb in pair:
+                        nc.tensor.matmul(
+                            hid_ps[db][:],
+                            w_pool_sb[:, cb, db * PARTS : (db + 1) * PARTS],
+                            pooled_bf[cb][:],
+                            start=(cb == 0),
+                            stop=(cb == C_BLOCKS - 1),
+                        )
+
             for db in range(C_BLOCKS):
-                for cb in pair:
+                hid_pre = work.tile([PARTS, width], F32, name="hid_pre")
+                nc.scalar.activation(hid_pre[:], hid_ps[db][:], IDENTITY, bias=b_pool_sb[:, db : db + 1])
+                hid_bf = work.tile([PARTS, width], BF16, name="hid_bf")
+                nc.vector.scalar_tensor_tensor(hid_bf[:], hid_pre[:], SLOPE, hid_pre[:], MULT, MAX)
+                for mb in range(M_BLOCKS):
                     nc.tensor.matmul(
-                        hid_ps[db][:],
-                        w_pool_sb[:, cb, db * PARTS : (db + 1) * PARTS],
-                        pooled_bf[cb][:],
-                        start=(cb == 0),
-                        stop=(cb == C_BLOCKS - 1),
+                        out_ps[mb][:],
+                        w_cls_sb[:, db, mb * PARTS : (mb + 1) * PARTS],
+                        hid_bf[:],
+                        start=(db == 0),
+                        stop=(db == C_BLOCKS - 1),
                     )
 
-        for db in range(C_BLOCKS):
-            hid_pre = work.tile([PARTS, P], F32, name="hid_pre")
-            nc.scalar.activation(hid_pre[:], hid_ps[db][:], IDENTITY, bias=b_pool_sb[:, db : db + 1])
-            hid_bf = work.tile([PARTS, P], BF16, name="hid_bf")
-            nc.vector.scalar_tensor_tensor(hid_bf[:], hid_pre[:], SLOPE, hid_pre[:], MULT, MAX)
             for mb in range(M_BLOCKS):
-                nc.tensor.matmul(
-                    out_ps[mb][:],
-                    w_cls_sb[:, db, mb * PARTS : (mb + 1) * PARTS],
-                    hid_bf[:],
-                    start=(db == 0),
-                    stop=(db == C_BLOCKS - 1),
-                )
-
-        for mb in range(M_BLOCKS):
-            out_pre = work.tile([PARTS, P], F32, name="out_pre")
-            nc.scalar.activation(out_pre[:], out_ps[mb][:], IDENTITY, bias=b_cls_sb[:, mb : mb + 1])
-            out_sb = work.tile([PARTS, P], F32, name="out_sb")
-            nc.vector.scalar_tensor_tensor(out_sb[:], out_pre[:], SLOPE, out_pre[:], MULT, MAX)
-            nc.sync.dma_start(out[mb * PARTS : (mb + 1) * PARTS, :], out_sb[:])
+                out_pre = work.tile([PARTS, width], F32, name="out_pre")
+                nc.scalar.activation(out_pre[:], out_ps[mb][:], IDENTITY, bias=b_cls_sb[:, mb : mb + 1])
+                out_sb = work.tile([PARTS, width], F32, name="out_sb")
+                nc.vector.scalar_tensor_tensor(out_sb[:], out_pre[:], SLOPE, out_pre[:], MULT, MAX)
+                nc.sync.dma_start(out[mb * PARTS : (mb + 1) * PARTS, lo:hi], out_sb[:])

@@ -15,6 +15,7 @@ ADD = mybir.AluOpType.add
 MULT = mybir.AluOpType.mult
 MAX = mybir.AluOpType.max
 IDENTITY = mybir.ActivationFunctionType.Identity
+RELU = mybir.ActivationFunctionType.Relu
 
 CHUNKS = ((0, 384), (384, 512))
 
@@ -43,8 +44,14 @@ def tile_myclassifier_kernel(tc, x, w_pool, b_pool, w_cls, b_cls, offs, out):
             nc.sync.dma_start(b_pool_sb[:], b_pool.rearrange("(db p) one -> p (db one)", p=PARTS))
             nc.sync.dma_start(b_cls_sb[:], b_cls.rearrange("(mb p) one -> p (mb one)", p=PARTS))
 
+        w_cls_neg = held.tile([PARTS, C_BLOCKS, M], BF16, name="w_cls_neg")
+        nc.scalar.mul(w_cls_neg[:], w_cls_sb[:], -1.0)
+        b_pool_neg = held.tile([PARTS, C_BLOCKS], F32, name="b_pool_neg")
+        nc.scalar.mul(b_pool_neg[:], b_pool_sb[:], -SLOPE)
+
         for lo, hi in CHUNKS:
             width = hi - lo
+            gathers_go_on = hi < P
             hid_ps = [psum.tile([PARTS, width], F32, name=f"hid_ps{db}") for db in range(C_BLOCKS)]
             out_ps = [psum.tile([PARTS, width], F32, name=f"out_ps{mb}") for mb in range(M_BLOCKS)]
 
@@ -78,18 +85,29 @@ def tile_myclassifier_kernel(tc, x, w_pool, b_pool, w_cls, b_cls, offs, out):
                         )
 
             for db in range(C_BLOCKS):
-                hid_pre = work.tile([PARTS, width], F32, name="hid_pre")
-                nc.scalar.activation(hid_pre[:], hid_ps[db][:], IDENTITY, bias=b_pool_sb[:, db : db + 1])
-                hid_bf = work.tile([PARTS, width], BF16, name="hid_bf")
-                nc.vector.scalar_tensor_tensor(hid_bf[:], hid_pre[:], SLOPE, hid_pre[:], MULT, MAX)
-                for mb in range(M_BLOCKS):
-                    nc.tensor.matmul(
-                        out_ps[mb][:],
-                        w_cls_sb[:, db, mb * PARTS : (mb + 1) * PARTS],
-                        hid_bf[:],
-                        start=(db == 0),
-                        stop=(db == C_BLOCKS - 1),
+                if gathers_go_on:
+                    hid_pos = work.tile([PARTS, width], BF16, name="hid_pos")
+                    nc.scalar.activation(hid_pos[:], hid_ps[db][:], RELU, bias=b_pool_sb[:, db : db + 1])
+                    hid_neg = work.tile([PARTS, width], BF16, name="hid_neg")
+                    nc.scalar.activation(
+                        hid_neg[:], hid_ps[db][:], RELU, bias=b_pool_neg[:, db : db + 1], scale=-SLOPE
                     )
+                    terms = ((w_cls_sb, hid_pos), (w_cls_neg, hid_neg))
+                else:
+                    hid_pre = work.tile([PARTS, width], F32, name="hid_pre")
+                    nc.scalar.activation(hid_pre[:], hid_ps[db][:], IDENTITY, bias=b_pool_sb[:, db : db + 1])
+                    hid_bf = work.tile([PARTS, width], BF16, name="hid_bf")
+                    nc.vector.scalar_tensor_tensor(hid_bf[:], hid_pre[:], SLOPE, hid_pre[:], MULT, MAX)
+                    terms = ((w_cls_sb, hid_bf),)
+                for mb in range(M_BLOCKS):
+                    for weights, term in terms:
+                        nc.tensor.matmul(
+                            out_ps[mb][:],
+                            weights[:, db, mb * PARTS : (mb + 1) * PARTS],
+                            term[:],
+                            start=(db == 0 and term is terms[0][1]),
+                            stop=(db == C_BLOCKS - 1 and term is terms[-1][1]),
+                        )
 
             for mb in range(M_BLOCKS):
                 out_pre = work.tile([PARTS, width], F32, name="out_pre")

@@ -17,7 +17,7 @@ MAX = mybir.AluOpType.max
 IDENTITY = mybir.ActivationFunctionType.Identity
 RELU = mybir.ActivationFunctionType.Relu
 
-CHUNKS = ((0, 384), (384, 512))
+CHUNKS = ((0, 352), (352, 512))
 
 
 def tile_myclassifier_kernel(tc, x, w_pool, b_pool, w_cls, b_cls, offs, out):
@@ -49,12 +49,9 @@ def tile_myclassifier_kernel(tc, x, w_pool, b_pool, w_cls, b_cls, offs, out):
         b_pool_neg = held.tile([PARTS, C_BLOCKS], F32, name="b_pool_neg")
         nc.scalar.mul(b_pool_neg[:], b_pool_sb[:], -SLOPE)
 
-        for lo, hi in CHUNKS:
+        def pool_and_project(lo, hi):
             width = hi - lo
-            gathers_go_on = hi < P
             hid_ps = [psum.tile([PARTS, width], F32, name=f"hid_ps{db}") for db in range(C_BLOCKS)]
-            out_ps = [psum.tile([PARTS, width], F32, name=f"out_ps{mb}") for mb in range(M_BLOCKS)]
-
             for first in range(0, C_BLOCKS, 2):
                 pair = (first, first + 1)
                 pooled = {}
@@ -83,9 +80,13 @@ def tile_myclassifier_kernel(tc, x, w_pool, b_pool, w_cls, b_cls, offs, out):
                             start=(cb == 0),
                             stop=(cb == C_BLOCKS - 1),
                         )
+            return hid_ps
 
+        def hidden_and_classify(lo, hi, hid_ps):
+            width = hi - lo
+            out_ps = [psum.tile([PARTS, width], F32, name=f"out_ps{mb}") for mb in range(M_BLOCKS)]
             for db in range(C_BLOCKS):
-                if gathers_go_on:
+                if hi < P:
                     hid_pos = work.tile([PARTS, width], BF16, name="hid_pos")
                     nc.scalar.activation(hid_pos[:], hid_ps[db][:], RELU, bias=b_pool_sb[:, db : db + 1])
                     hid_neg = work.tile([PARTS, width], BF16, name="hid_neg")
@@ -108,10 +109,16 @@ def tile_myclassifier_kernel(tc, x, w_pool, b_pool, w_cls, b_cls, offs, out):
                             start=(db == 0 and term is terms[0][1]),
                             stop=(db == C_BLOCKS - 1 and term is terms[-1][1]),
                         )
+            return out_ps
 
+        def finish(lo, hi, out_ps):
+            width = hi - lo
             for mb in range(M_BLOCKS):
                 out_pre = work.tile([PARTS, width], F32, name="out_pre")
                 nc.scalar.activation(out_pre[:], out_ps[mb][:], IDENTITY, bias=b_cls_sb[:, mb : mb + 1])
                 out_sb = work.tile([PARTS, width], F32, name="out_sb")
                 nc.vector.scalar_tensor_tensor(out_sb[:], out_pre[:], SLOPE, out_pre[:], MULT, MAX)
                 nc.sync.dma_start(out[mb * PARTS : (mb + 1) * PARTS, lo:hi], out_sb[:])
+
+        for lo, hi in CHUNKS:
+            finish(lo, hi, hidden_and_classify(lo, hi, pool_and_project(lo, hi)))

@@ -35,7 +35,9 @@ def tile_myclassifier_kernel(tc, x, w_pool, b_pool, w_cls, b_cls, offs, out):
         w_cls_sb = held.tile([PARTS, C_BLOCKS, M], BF16, name="w_cls_sb")
         b_pool_sb = held.tile([PARTS, C_BLOCKS], F32, name="b_pool_sb")
         b_cls_sb = held.tile([PARTS, M_BLOCKS], F32, name="b_cls_sb")
-        for cb in range(C_BLOCKS):
+        nc.scalar.dma_start(tokens[0][:, S // 2 : S], x[0:PARTS, S // 2 : S])
+        nc.sync.dma_start(tokens[0][:, 0 : S // 2], x[0:PARTS, 0 : S // 2])
+        for cb in range(1, C_BLOCKS):
             nc.sync.dma_start(tokens[cb][:], x[cb * PARTS : (cb + 1) * PARTS, :])
             if cb == 1:
                 nc.sync.dma_start(w_pool_sb[:], w_pool.rearrange("(cb p) d -> p cb d", p=PARTS))

@@ -117,7 +117,10 @@ def tile_myclassifier_kernel(tc, x, w_pool, b_pool, w_cls, b_cls, offs, out):
             width = hi - lo
             for mb in range(M_BLOCKS):
                 out_pre = work.tile([PARTS, width], F32, name="out_pre")
-                nc.scalar.activation(out_pre[:], out_ps[mb][:], IDENTITY, bias=b_cls_sb[:, mb : mb + 1])
+                if hi < P:
+                    nc.vector.tensor_scalar_add(out_pre[:], out_ps[mb][:], b_cls_sb[:, mb : mb + 1])
+                else:
+                    nc.scalar.activation(out_pre[:], out_ps[mb][:], IDENTITY, bias=b_cls_sb[:, mb : mb + 1])
                 out_sb = work.tile([PARTS, width], F32, name="out_sb")
                 nc.vector.scalar_tensor_tensor(out_sb[:], out_pre[:], SLOPE, out_pre[:], MULT, MAX)
                 nc.sync.dma_start(out[mb * PARTS : (mb + 1) * PARTS, lo:hi], out_sb[:])

@@ -117,10 +117,7 @@ def tile_myclassifier_kernel(tc, x, w_pool, b_pool, w_cls, b_cls, offs, out):
             width = hi - lo
             for mb in range(M_BLOCKS):
                 out_pre = work.tile([PARTS, width], F32, name="out_pre")
-                if hi < P:
-                    nc.vector.tensor_scalar_add(out_pre[:], out_ps[mb][:], b_cls_sb[:, mb : mb + 1])
-                else:
-                    nc.scalar.activation(out_pre[:], out_ps[mb][:], IDENTITY, bias=b_cls_sb[:, mb : mb + 1])
+                nc.vector.tensor_scalar_add(out_pre[:], out_ps[mb][:], b_cls_sb[:, mb : mb + 1])
                 out_sb = work.tile([PARTS, width], F32, name="out_sb")
                 nc.vector.scalar_tensor_tensor(out_sb[:], out_pre[:], SLOPE, out_pre[:], MULT, MAX)
                 nc.sync.dma_start(out[mb * PARTS : (mb + 1) * PARTS, lo:hi], out_sb[:])

import concourse.mybir as mybir

C, S, P, L, M, N = 768, 1024, 512, 4, 256, 2048
SLOPE = 0.01
PARTS = 128
C_BLOCKS = C // PARTS
M_BLOCKS = M // PARTS
PIECE = P // 16
FLOPS = 2 * C * C * P + 2 * C * M * P

F32 = mybir.dt.float32
BF16 = mybir.dt.bfloat16
U16 = mybir.dt.uint16
ADD = mybir.AluOpType.add
MULT = mybir.AluOpType.mult
MAX = mybir.AluOpType.max
IDENTITY = mybir.ActivationFunctionType.Identity
RELU = mybir.ActivationFunctionType.Relu

CHUNKS = ((0, 352), (352, 512))


def tile_myclassifier_kernel(tc, x, w_pool, b_pool, w_cls, b_cls, offs, out):
    nc = tc.nc
    with (
        tc.tile_pool(name="held", bufs=1) as held,
        tc.tile_pool(name="sums", bufs=8) as sums,
        tc.tile_pool(name="work", bufs=6) as work,
        tc.psum_pool(name="psum", bufs=1) as psum,
    ):
        offsets = held.tile([PARTS, N // 16], U16, name="offsets")
        nc.sync.dma_start(offsets[:], offs)
        tokens = [held.tile([PARTS, S], F32, name=f"tokens{cb}") for cb in range(C_BLOCKS)]
        w_pool_sb = held.tile([PARTS, C_BLOCKS, C], BF16, name="w_pool_sb")
        w_cls_sb = held.tile([PARTS, C_BLOCKS, M], BF16, name="w_cls_sb")
        b_pool_sb = held.tile([PARTS, C_BLOCKS], F32, name="b_pool_sb")
        b_cls_sb = held.tile([PARTS, M_BLOCKS], F32, name="b_cls_sb")
        nc.scalar.dma_start(tokens[0][:, S // 2 : S], x[0:PARTS, S // 2 : S])
        nc.sync.dma_start(tokens[0][:, 0 : S // 2], x[0:PARTS, 0 : S // 2])
        for cb in range(1, C_BLOCKS):
            nc.sync.dma_start(tokens[cb][:], x[cb * PARTS : (cb + 1) * PARTS, :])
            if cb == 1:
                nc.sync.dma_start(w_pool_sb[:], w_pool.rearrange("(cb p) d -> p cb d", p=PARTS))
        nc.sync.dma_start(w_cls_sb[:], w_cls.rearrange("(db p) m -> p db m", p=PARTS))
        with nc.allow_non_contiguous_dma(reason="a bias value for each partition"):
            nc.sync.dma_start(b_pool_sb[:], b_pool.rearrange("(db p) one -> p (db one)", p=PARTS))
            nc.sync.dma_start(b_cls_sb[:], b_cls.rearrange("(mb p) one -> p (mb one)", p=PARTS))

        w_cls_neg = held.tile([PARTS, C_BLOCKS, M], BF16, name="w_cls_neg")
        nc.scalar.mul(w_cls_neg[:], w_cls_sb[:], -1.0)
        b_pool_neg = held.tile([PARTS, C_BLOCKS], F32, name="b_pool_neg")
        nc.scalar.mul(b_pool_neg[:], b_pool_sb[:], -SLOPE)

        def pool_and_project(lo, hi):
            width = hi - lo
            hid_ps = [psum.tile([PARTS, width], F32, name=f"hid_ps{db}") for db in range(C_BLOCKS)]
            for first in range(0, C_BLOCKS, 2):
                pair = (first, first + 1)
                pooled = {}
                for cb in pair:
                    pooled[cb] = sums.tile([PARTS, width], F32, name="pooled")
                    picked = tokens[cb][:].indirect(offsets[:, lo // 16 : hi // 16])
                    nc.vector.tensor_copy(pooled[cb][:], picked)
                for l in range(1, L):
                    for cb in pair:
                        shorter = pooled[cb]
                        pooled[cb] = sums.tile([PARTS, width], F32, name="pooled")
                        picked = tokens[cb][:].indirect(
                            offsets[:, l * PIECE + lo // 16 : l * PIECE + hi // 16]
                        )
                        nc.vector.tensor_tensor(pooled[cb][:], picked, shorter[:], ADD)
                pooled_bf = {}
                for cb in pair:
                    pooled_bf[cb] = work.tile([PARTS, width], BF16, name="pooled_bf")
                    nc.scalar.copy(pooled_bf[cb][:], pooled[cb][:])
                for db in range(C_BLOCKS):
                    for cb in pair:
                        nc.tensor.matmul(
                            hid_ps[db][:],
                            w_pool_sb[:, cb, db * PARTS : (db + 1) * PARTS],
                            pooled_bf[cb][:],
                            start=(cb == 0),
                            stop=(cb == C_BLOCKS - 1),
                        )
            return hid_ps

        def hidden_and_classify(lo, hi, hid_ps):
            width = hi - lo
            out_ps = [psum.tile([PARTS, width], F32, name=f"out_ps{mb}") for mb in range(M_BLOCKS)]
            for db in range(C_BLOCKS):
                if hi < P:
                    hid_pos = work.tile([PARTS, width], BF16, name="hid_pos")
                    nc.scalar.activation(hid_pos[:], hid_ps[db][:], RELU, bias=b_pool_sb[:, db : db + 1])
                    hid_neg = work.tile([PARTS, width], BF16, name="hid_neg")
                    nc.scalar.activation(
                        hid_neg[:], hid_ps[db][:], RELU, bias=b_pool_neg[:, db : db + 1], scale=-SLOPE
                    )
                    terms = ((w_cls_sb, hid_pos), (w_cls_neg, hid_neg))
                else:
                    hid_pre = work.tile([PARTS, width], F32, name="hid_pre")
                    nc.scalar.activation(hid_pre[:], hid_ps[db][:], IDENTITY, bias=b_pool_sb[:, db : db + 1])
                    hid_bf = work.tile([PARTS, width], BF16, name="hid_bf")
                    nc.vector.scalar_tensor_tensor(hid_bf[:], hid_pre[:], SLOPE, hid_pre[:], MULT, MAX)
                    terms = ((w_cls_sb, hid_bf),)
                for mb in range(M_BLOCKS):
                    for weights, term in terms:
                        nc.tensor.matmul(
                            out_ps[mb][:],
                            weights[:, db, mb * PARTS : (mb + 1) * PARTS],
                            term[:],
                            start=(db == 0 and term is terms[0][1]),
                            stop=(db == C_BLOCKS - 1 and term is terms[-1][1]),
                        )
            return out_ps

        def finish(lo, hi, out_ps):
            width = hi - lo
            for mb in range(M_BLOCKS):
                out_pre = work.tile([PARTS, width], F32, name="out_pre")
                nc.vector.tensor_scalar_add(out_pre[:], out_ps[mb][:], b_cls_sb[:, mb : mb + 1])
                out_sb = work.tile([PARTS, width], F32, name="out_sb")
                nc.vector.scalar_tensor_tensor(out_sb[:], out_pre[:], SLOPE, out_pre[:], MULT, MAX)
                nc.sync.dma_start(out[mb * PARTS : (mb + 1) * PARTS, lo:hi], out_sb[:])

        for lo, hi in CHUNKS:
            finish(lo, hi, hidden_and_classify(lo, hi, pool_and_project(lo, hi)))
